import numpy as np
import ml_dtypes


def mxq(x, axis, fmt="e4m3"):
    dtype, down = {"e4m3": (ml_dtypes.float8_e4m3fn, 7), "e5m2": (ml_dtypes.float8_e5m2, 14)}[fmt]
    v = np.moveaxis(np.asarray(x, np.float32).astype(ml_dtypes.bfloat16).astype(np.float64), axis, -1)
    blocks = v.reshape(v.shape[:-1] + (-1, 32))
    amax = np.abs(blocks).max(-1, keepdims=True)
    byte = np.maximum(np.where(amax > 0, np.frexp(amax)[1] - 1 + 127, 0) - down, 1)
    scale = np.exp2(byte - 127.0)
    codes = (blocks / scale).astype(np.float32).astype(dtype).astype(np.float64)
    return np.moveaxis((codes * scale).reshape(v.shape), -1, axis)


WIDE = False


def mx_kscale(k):
    if not WIDE:
        return np.ones(k)
    levels = np.array([10, -10, 5, -5, 0])
    if k % 512:
        return np.exp2(np.random.permutation(np.resize(levels, k // 32))).repeat(32)
    a = np.empty((k // 512, 16))
    for p in range(k // 512):
        a[p, :8] = np.random.permutation(np.resize(levels, 8))
        for g in range(8):
            far = levels[np.abs(levels - a[p, g]) >= 10]
            a[p, g + 8] = far[np.random.randint(len(far))]
    return np.exp2(a.ravel()).repeat(32)


BF16 = ml_dtypes.bfloat16


def bf(x):
    return np.asarray(x, np.float32).astype(BF16)


def f64(x):
    return np.asarray(x).astype(np.float64)


B, K, N = 1024, 2048, 2048
EPS = 1e-5
GELU_C = 0.7978845608


def setup_inputs():
    s = mx_kscale(K)
    return {"x": bf(np.random.standard_normal((B, K)) * s),
            "weight": bf(np.random.standard_normal((K, N)) * np.sqrt(2.0 / K) / s[:, None]),
            "bn_gamma": bf(np.random.uniform(0.5, 1.5, N)),
            "bn_beta": bf(np.random.standard_normal(N) * 0.1),
            "bn_mean": bf(np.random.standard_normal(N) * 0.1),
            "bn_var": bf(np.random.uniform(0.5, 1.5, N))}


def core(x, weight, bn_gamma, bn_beta, bn_mean, bn_var):
    acc = mxq(f64(x), 1, "e4m3") @ mxq(f64(weight), 0, "e4m3")
    x_norm = (acc - f64(bn_mean)) / np.sqrt(f64(bn_var) + EPS)
    bn_out = f64(bn_gamma) * x_norm + f64(bn_beta)
    gelu = 0.5 * bn_out * (1.0 + np.tanh(GELU_C * (bn_out + 0.044715 * bn_out * bn_out * bn_out)))
    return np.maximum(gelu, 0.0)


def e4m3fn_bytes(y):
    return np.clip(np.asarray(y, np.float64), -448.0, 448.0).astype(np.float32).astype(ml_dtypes.float8_e4m3fn).view(np.uint8)


def reference(x, weight, bn_gamma, bn_beta, bn_mean, bn_var):
    out = core(x, weight, bn_gamma, bn_beta, bn_mean, bn_var)
    s = np.max(np.abs(out)) / 448.0
    return out, e4m3fn_bytes(out / s)

@@ -1,0 +1,353 @@
+from contextlib import ExitStack
+
+import concourse.masks as masks
+import concourse.mybir as mybir
+
+B, K, N = 1024, 2048, 2048
+EPS = 1e-5
+FLOPS = 2 * B * K * N
+
+F32 = mybir.dt.float32
+BF16 = mybir.dt.bfloat16
+U32 = mybir.dt.uint32
+U8 = mybir.dt.uint8
+FP8X4 = mybir.dt.float8_e4m3fn_x4
+FP8 = mybir.dt.float8_e4m3fn
+ALU = mybir.AluOpType
+ACT = mybir.ActivationFunctionType
+AX = mybir.AxisListType
+
+P = 128
+G = K // 512
+NI = B // P
+NJ = N // P
+WC = 256
+NC = N // WC
+
+
+def tile_modelnew_kernel(tc, x, weight, bn_gamma, bn_beta, bn_mean, bn_var, out_0, out_1):
+    nc = tc.nc
+    x_v = x.rearrange("(p i) k -> p i k", i=NI)
+    w_v = weight.rearrange("(g p j) n -> g p j n", g=G, j=4)
+    o0_v = out_0.rearrange("(p i) n -> p i n", i=NI)
+    o1_v = out_1.rearrange("(p i) n -> p (i n)", i=NI)
+
+    with ExitStack() as ctx:
+        const = ctx.enter_context(tc.tile_pool(name="const", bufs=1))
+        acc_pool = ctx.enter_context(tc.psum_pool(name="accp", bufs=4))
+        tp_pool = ctx.enter_context(tc.psum_pool(name="tpp", bufs=4))
+        ctx.enter_context(tc.manual_schedule())
+
+        out_sb = const.tile([P, NC, NI, WC], F32, name="out_sb")
+        stat = const.tile([P, 2 * NJ], F32, name="stat")
+        ident_f = const.tile([P, P], F32, name="ident_f")
+        ident_b = const.tile([P, P], BF16, name="ident_b")
+        prm = const.tile([P, P], BF16, name="prm")
+        prm_t = const.tile([P, 64], F32, name="prm_t")
+        neg_half = const.tile([P, NJ], F32, name="neg_half")
+        var_eps = const.tile([P, NJ], F32, name="var_eps")
+        rstd = const.tile([P, NJ], F32, name="rstd")
+        a_col = const.tile([P, NJ], F32, name="a_col")
+        ma_col = const.tile([P, NJ], F32, name="ma_col")
+        c_col = const.tile([P, NJ], F32, name="c_col")
+        warm_in = const.tile([P, 1], F32, name="warm_in")
+        warm_out = const.tile([P, 1], F32, name="warm_out")
+        pmax = const.tile([P, 1], F32, name="pmax")
+        junk = const.tile([P, P], F32, name="junk")
+        sfac = const.tile([P, 1], F32, name="sfac")
+        rfac = const.tile([P, 1], F32, name="rfac")
+
+        for v, vec in enumerate((bn_gamma, bn_beta, bn_mean, bn_var)):
+            nc.sync.dma_start(out=prm[16 * v : 16 * (v + 1), :], in_=vec.rearrange("(j c) -> j c", c=P))
+        nc.vector.memset(warm_in[:], 0.0)
+        nc.scalar.activation(out=warm_out[:], in_=warm_in[:], func=ACT.Gelu_apprx_tanh)
+        nc.gpsimd.memset(prm[64:128, :], 0.0)
+        masks.make_identity(nc, ident_b[:])
+        masks.make_identity(nc, ident_f[:])
+        nc.gpsimd.memset(neg_half[:], -0.5)
+
+        with ExitStack() as ph1:
+            xraw_pool = ph1.enter_context(tc.tile_pool(name="xrawp", bufs=NI))
+            xg_pool = ph1.enter_context(tc.tile_pool(name="xgp", bufs=2))
+            xc_pool = ph1.enter_context(tc.tile_pool(name="xcp", bufs=1))
+            wraw_pool = ph1.enter_context(tc.tile_pool(name="wrawp", bufs=16))
+            wgrp_pool = ph1.enter_context(tc.tile_pool(name="wgrpp", bufs=6))
+            wc_pool = ph1.enter_context(tc.tile_pool(name="wcp", bufs=3))
+            g_pool = ph1.enter_context(tc.tile_pool(name="gp", bufs=6))
+
+            xc = [xc_pool.tile([P, G, 512], U32, name="xc%d" % h, align_bytes=64) for h in range(2)]
+            xs = [xc_pool.tile([P, G, 512], U8, name="xs%d" % h, align_bytes=64) for h in range(2)]
+            xraw = {}
+            xg = {}
+            wraw = {}
+            wgrp = {}
+            wc = {}
+            ws = {}
+            acc = {}
+            gt = {}
+
+            def load_x(i):
+                t = xraw_pool.tile([P, K], BF16, name="xraw", tag="xraw")
+                nc.sync.dma_start(out=t[:], in_=x_v[:, i, :])
+                xraw[i] = t
+
+            def load_w(c):
+                for g in range(G):
+                    t = wraw_pool.tile([P, 4, WC], BF16, name="wraw", tag="wraw")
+                    nc.sync.dma_start(out=t[:], in_=w_v[g, :, :, WC * c : WC * (c + 1)])
+                    wraw[(c, g)] = t
+
+            def xt(i):
+                q, il = divmod(i, 2)
+                if il == 0:
+                    xg[q] = xg_pool.tile([P, G, 2, 512], BF16, name="xg", tag="xg", align_bytes=64)
+                words = xraw[i][:].bitcast(F32)
+                for gp in range(2):
+                    bank = tp_pool.tile([P, 512], F32, name="tp", tag="tp")
+                    for g2 in range(2):
+                        for u in range(2):
+                            g = 2 * gp + g2
+                            s = 2 * g2 + u
+                            nc.tensor.transpose(
+                                bank[:, P * s : P * (s + 1)],
+                                words[:, 256 * g + u : 256 * (g + 1) : 2],
+                                ident_f[:],
+                            )
+                    dst = xg[q][:, 2 * gp : 2 * gp + 2, il, :].bitcast(F32).rearrange("p g (r u) -> p g r u", u=2)
+                    src = bank[:].rearrange("p (g u r) -> p g r u", g=2, u=2)
+                    if gp == 0 and i < 4:
+                        nc.vector.tensor_copy(out=dst, in_=src)
+                    else:
+                        nc.scalar.copy(out=dst, in_=src)
+
+            def xq(q):
+                h, half = divmod(q, 2)
+                cols = slice(256 * half, 256 * (half + 1))
+                for g in range(G):
+                    nc.vector.quantize_mx(
+                        out=xc[h][:, g, cols].bitcast(FP8X4),
+                        scales=xs[h][:, g, cols],
+                        in_=xg[q][:, g, :, :].rearrange("p l c -> p (l c)"),
+                    )
+
+            def wcopy(c, g, on_vector=None):
+                if c >= NC:
+                    return
+                if on_vector is None:
+                    on_vector = g % 2 == 1
+                t = wgrp_pool.tile([P, WC, 4], BF16, name="wgrp", tag="wgrp", align_bytes=64)
+                src = wraw[(c, g)][:].rearrange("p j n -> p n j")
+                if on_vector:
+                    nc.vector.tensor_copy(out=t[:], in_=src)
+                else:
+                    nc.scalar.copy(out=t[:], in_=src)
+                wgrp[(c, g)] = t
+
+            def wquant(c, g):
+                if c >= NC:
+                    return
+                if g == 0:
+                    wc[c] = wc_pool.tile([P, G, WC], U32, name="wc", tag="wc", align_bytes=64)
+                    ws[c] = wc_pool.tile([P, G, WC], U8, name="ws", tag="ws", align_bytes=64)
+                nc.vector.quantize_mx(
+                    out=wc[c][:, g, :].bitcast(FP8X4),
+                    scales=ws[c][:, g, :],
+                    in_=wgrp[(c, g)][:].rearrange("p n j -> p (n j)"),
+                )
+                if g == G - 1 and c + 4 < NC:
+                    load_w(c + 4)
+
+            def mx(j, h):
+                c, s = divmod(j, 2)
+                cols = slice(P * s, P * (s + 1))
+                a = acc_pool.tile([P, 512], F32, name="acc", tag="acc")
+                for g in range(G):
+                    nc.tensor.matmul_mx(
+                        out=a[:],
+                        lhsT=wc[c][:, g, cols].bitcast(FP8X4),
+                        lhsT_scale=ws[c][:, g, cols],
+                        rhs=xc[h][:, g, :].bitcast(FP8X4),
+                        rhs_scale=xs[h][:, g, :],
+                        start=(g == 0),
+                        stop=(g == G - 1),
+                    )
+                t = g_pool.tile([P, 512], F32, name="gt", tag="gt")
+                nc.scalar.activation(
+                    out=t[:],
+                    in_=a[:],
+                    func=ACT.Gelu_apprx_tanh,
+                    bias=c_col[:, j : j + 1],
+                    scale=a_col[:, j : j + 1],
+                )
+                gt[(j, h)] = t
+
+            def tr(j, h):
+                c, s = divmod(j, 2)
+                bank = tp_pool.tile([P, 512], F32, name="tp", tag="tp")
+                for q in range(4):
+                    nc.tensor.transpose(bank[:, P * q : P * (q + 1)], gt[(j, h)][:, P * q : P * (q + 1)], ident_f[:])
+                nc.vector.tensor_scalar(
+                    out=out_sb[:, c, 4 * h : 4 * h + 4, P * s : P * (s + 1)],
+                    in0=bank[:].rearrange("p (q n) -> p q n", q=4),
+                    scalar1=0.0,
+                    scalar2=None,
+                    op0=ALU.max,
+                    op1=ALU.max,
+                    accum_out=stat[:, 2 * j + h : 2 * j + h + 1],
+                )
+                if s == 1 and h == 1:
+                    nc.sync.dma_start(out=o0_v[:, :, WC * c : WC * (c + 1)], in_=out_sb[:, c, :, :])
+
+            for i in range(4):
+                load_x(i)
+            load_w(0)
+            for i in range(4, NI):
+                load_x(i)
+            for c in range(1, 4):
+                load_w(c)
+
+            prm_ps = tp_pool.tile([P, P], BF16, name="tp", tag="tp")
+            nc.tensor.transpose(prm_ps[:], prm[:], ident_b[:])
+            nc.vector.tensor_copy(out=prm_t[:], in_=prm_ps[:, 0:64])
+            nc.vector.tensor_scalar(out=var_eps[:], in0=prm_t[:, 48:64], scalar1=EPS, scalar2=None, op0=ALU.add)
+            nc.gpsimd.tensor_tensor(out=rstd[:], in0=var_eps[:], in1=neg_half[:], op=ALU.pow)
+
+            xt(0)
+            xt(1)
+            xq(0)
+            xt(2)
+            xt(3)
+            nc.vector.tensor_tensor(out=a_col[:], in0=prm_t[:, 0:16], in1=rstd[:], op=ALU.mult)
+            wcopy(0, 0)
+            wcopy(0, 1)
+            nc.vector.tensor_tensor(out=ma_col[:], in0=prm_t[:, 32:48], in1=a_col[:], op=ALU.mult)
+            xq(1)
+            nc.vector.tensor_tensor(out=c_col[:], in0=prm_t[:, 16:32], in1=ma_col[:], op=ALU.subtract)
+            wcopy(0, 2)
+            wquant(0, 0)
+            wquant(0, 1)
+            wcopy(0, 3)
+            wquant(0, 2)
+            wquant(0, 3)
+            mx(0, 0)
+            mx(1, 0)
+            xt(4)
+            xt(5)
+            wcopy(1, 0, True)
+            wcopy(1, 1, True)
+            xq(2)
+            xt(6)
+            xt(7)
+            wcopy(1, 2, True)
+            xq(3)
+            wcopy(1, 3, True)
+            wquant(1, 0)
+            wquant(1, 1)
+            wquant(1, 2)
+            wquant(1, 3)
+            tr(0, 0)
+            tr(1, 0)
+            mx(0, 1)
+            mx(1, 1)
+            wcopy(2, 0)
+            wcopy(2, 1)
+            for j in range(2, NJ):
+                mx(j, 0)
+                mx(j, 1)
+                c = j // 2 + 1
+                if j % 2 == 0:
+                    wcopy(c, 2)
+                    wcopy(c, 3)
+                    wquant(c, 0)
+                    wquant(c, 1)
+                else:
+                    wcopy(c + 1, 0)
+                    wcopy(c + 1, 1)
+                    wquant(c, 2)
+                    wquant(c, 3)
+                if j == 2:
+                    tr(0, 1)
+                    tr(1, 1)
+                else:
+                    tr(j - 1, 0)
+                    tr(j - 1, 1)
+            tr(NJ - 1, 0)
+            tr(NJ - 1, 1)
+
+        nc.vector.tensor_reduce(out=pmax[:], in_=stat[:], axis=AX.X, op=ALU.max)
+        spread = tp_pool.tile([P, P], F32, name="tp", tag="tp")
+        nc.tensor.transpose(spread[:], pmax[:, 0:1].to_broadcast([P, P]), ident_f[:])
+        nc.vector.tensor_scalar(
+            out=junk[:], in0=spread[:], scalar1=1.0 / 448.0, scalar2=None, op0=ALU.mult, op1=ALU.max, accum_out=sfac[:]
+        )
+        nc.vector.reciprocal(out=rfac[:], in_=sfac[:])
+
+        with ExitStack() as ph2:
+            sc_pool = ph2.enter_context(tc.tile_pool(name="scp", bufs=3))
+            f8_pool = ph2.enter_context(tc.tile_pool(name="f8p", bufs=NI))
+            f8 = [f8_pool.tile([P, N], FP8, name="f8", tag="f8") for r in range(NI)]
+            work_v = [(r, 0, NC) for r in range(5)] + [(7, 0, 3)]
+            work_s = [(5, 0, NC), (6, 0, NC), (7, 3, NC)]
+            sc_v = {}
+            sc_s = {}
+
+            def scale_v(k):
+                r, c0, c1 = work_v[k]
+                t = sc_pool.tile([P, (c1 - c0) * WC], F32, name="scv", tag="scv")
+                nc.vector.tensor_scalar(
+                    out=t[:].rearrange("p (c n) -> p c n", n=WC),
+                    in0=out_sb[:, c0:c1, r, :],
+                    scalar1=rfac[:, 0:1],
+                    scalar2=None,
+                    op0=ALU.mult,
+                )
+                sc_v[k] = t
+
+            def scale_s(k):
+                r, c0, c1 = work_s[k]
+                t = sc_pool.tile([P, (c1 - c0) * WC], F32, name="scs", tag="scs")
+                nc.scalar.activation(
+                    out=t[:].rearrange("p (c n) -> p c n", n=WC),
+                    in_=out_sb[:, c0:c1, r, :],
+                    func=ACT.Copy,
+                    scale=rfac[:, 0:1],
+                )
+                sc_s[k] = t
+
+            def cast_v(k):
+                r, c0, c1 = work_v[k]
+                nc.vector.tensor_copy(out=f8[r][:, WC * c0 : WC * c1], in_=sc_v[k][:], saturate=False)
+
+            def cast_s(k):
+                r, c0, c1 = work_s[k]
+                nc.scalar.copy(out=f8[r][:, WC * c0 : WC * c1], in_=sc_s[k][:], saturate=False)
+
+            def store1(r):
+                nc.sync.dma_start(out=o1_v[:, N * r : N * (r + 1)], in_=f8[r][:].bitcast(U8))
+
+            scale_v(0)
+            scale_s(0)
+            scale_v(1)
+            cast_v(0)
+            store1(0)
+            scale_s(1)
+            scale_v(2)
+            cast_v(1)
+            store1(1)
+            cast_s(0)
+            store1(5)
+            scale_v(3)
+            cast_v(2)
+            store1(2)
+            scale_s(2)
+            scale_v(4)
+            cast_v(3)
+            store1(3)
+            cast_s(1)
+            store1(6)
+            scale_v(5)
+            cast_v(4)
+            store1(4)
+            cast_s(2)
+            cast_v(5)
+            store1(7)

@@ -56,9 +56,11 @@ def tile_modelnew_kernel(tc, x, weight, bn_gamma, bn_beta, bn_mean, bn_var, out_
         junk = const.tile([P, P], F32, name="junk")
         sfac = const.tile([P, 1], F32, name="sfac")
         rfac = const.tile([P, 1], F32, name="rfac")
+        zero_bf = const.tile([P, 512], BF16, name="zero_bf")
 
         for v, vec in enumerate((bn_gamma, bn_beta, bn_mean, bn_var)):
             nc.sync.dma_start(out=prm[16 * v : 16 * (v + 1), :], in_=vec.rearrange("(j c) -> j c", c=P))
+        nc.vector.memset(zero_bf[:], 0.0)
         nc.vector.memset(warm_in[:], 0.0)
         nc.scalar.activation(out=warm_out[:], in_=warm_in[:], func=ACT.Gelu_apprx_tanh)
         nc.gpsimd.memset(prm[64:128, :], 0.0)
@@ -68,6 +70,7 @@ def tile_modelnew_kernel(tc, x, weight, bn_gamma, bn_beta, bn_mean, bn_var, out_
 
         with ExitStack() as ph1:
             xraw_pool = ph1.enter_context(tc.tile_pool(name="xrawp", bufs=NI))
+            xr_pool = ph1.enter_context(tc.tile_pool(name="xrp", bufs=4))
             xg_pool = ph1.enter_context(tc.tile_pool(name="xgp", bufs=2))
             xc_pool = ph1.enter_context(tc.tile_pool(name="xcp", bufs=1))
             wraw_pool = ph1.enter_context(tc.tile_pool(name="wrawp", bufs=16))
@@ -78,13 +81,14 @@ def tile_modelnew_kernel(tc, x, weight, bn_gamma, bn_beta, bn_mean, bn_var, out_
             xc = [xc_pool.tile([P, G, 512], U32, name="xc%d" % h, align_bytes=64) for h in range(2)]
             xs = [xc_pool.tile([P, G, 512], U8, name="xs%d" % h, align_bytes=64) for h in range(2)]
             xraw = {}
+            xr = {}
             xg = {}
             wraw = {}
             wgrp = {}
             wc = {}
             ws = {}
-            acc = {}
             gt = {}
+            done = []
 
             def load_x(i):
                 t = xraw_pool.tile([P, K], BF16, name="xraw", tag="xraw")
@@ -97,7 +101,22 @@ def tile_modelnew_kernel(tc, x, weight, bn_gamma, bn_beta, bn_mean, bn_var, out_
                     nc.sync.dma_start(out=t[:], in_=w_v[g, :, :, WC * c : WC * (c + 1)])
                     wraw[(c, g)] = t
 
-            def xt(i):
+            def spin(n):
+                if n == 0:
+                    return
+                t = acc_pool.tile([P, 512], F32, name="acc", tag="acc")
+                for k in range(n):
+                    nc.tensor.matmul(out=t[:], lhsT=zero_bf[:, 0:P], rhs=zero_bf[:], start=True, stop=True)
+
+            def xorder(i):
+                t = xr_pool.tile([P, K // 2], F32, name="xr", tag="xr")
+                nc.vector.tensor_copy(
+                    out=t[:].rearrange("p (g u m) -> p g u m", g=G, u=2),
+                    in_=xraw[i][:].bitcast(F32).rearrange("p (g m u) -> p g u m", g=G, u=2),
+                )
+                xr[i] = t
+
+            def xt(i, both_on_scalar):
                 q, il = divmod(i, 2)
                 if il == 0:
                     xg[q] = xg_pool.tile([P, G, 2, 512], BF16, name="xg", tag="xg", align_bytes=64)
@@ -108,33 +127,30 @@ def tile_modelnew_kernel(tc, x, weight, bn_gamma, bn_beta, bn_mean, bn_var, out_
                         for u in range(2):
                             g = 2 * gp + g2
                             s = 2 * g2 + u
-                            nc.tensor.transpose(
-                                bank[:, P * s : P * (s + 1)],
-                                words[:, 256 * g + u : 256 * (g + 1) : 2],
-                                ident_f[:],
-                            )
+                            if i in xr:
+                                src_w = xr[i][:, P * (2 * g + u) : P * (2 * g + u + 1)]
+                            else:
+                                src_w = words[:, 256 * g + u : 256 * (g + 1) : 2]
+                            nc.tensor.transpose(bank[:, P * s : P * (s + 1)], src_w, ident_f[:])
                     dst = xg[q][:, 2 * gp : 2 * gp + 2, il, :].bitcast(F32).rearrange("p g (r u) -> p g r u", u=2)
                     src = bank[:].rearrange("p (g u r) -> p g r u", g=2, u=2)
-                    if gp == 0 and i < 4:
+                    if gp == 0 and not both_on_scalar:
                         nc.vector.tensor_copy(out=dst, in_=src)
                     else:
                         nc.scalar.copy(out=dst, in_=src)
 
-            def xq(q):
+            def xq(q, g):
                 h, half = divmod(q, 2)
                 cols = slice(256 * half, 256 * (half + 1))
-                for g in range(G):
-                    nc.vector.quantize_mx(
-                        out=xc[h][:, g, cols].bitcast(FP8X4),
-                        scales=xs[h][:, g, cols],
-                        in_=xg[q][:, g, :, :].rearrange("p l c -> p (l c)"),
-                    )
+                nc.vector.quantize_mx(
+                    out=xc[h][:, g, cols].bitcast(FP8X4),
+                    scales=xs[h][:, g, cols],
+                    in_=xg[q][:, g, :, :].rearrange("p l c -> p (l c)"),
+                )
 
-            def wcopy(c, g, on_vector=None):
+            def wcopy(c, g, on_vector):
                 if c >= NC:
                     return
-                if on_vector is None:
-                    on_vector = g % 2 == 1
                 t = wgrp_pool.tile([P, WC, 4], BF16, name="wgrp", tag="wgrp", align_bytes=64)
                 src = wraw[(c, g)][:].rearrange("p j n -> p n j")
                 if on_vector:
@@ -146,7 +162,7 @@ def tile_modelnew_kernel(tc, x, weight, bn_gamma, bn_beta, bn_mean, bn_var, out_
             def wquant(c, g):
                 if c >= NC:
                     return
-                if g == 0:
+                if c not in wc:
                     wc[c] = wc_pool.tile([P, G, WC], U32, name="wc", tag="wc", align_bytes=64)
                     ws[c] = wc_pool.tile([P, G, WC], U8, name="ws", tag="ws", align_bytes=64)
                 nc.vector.quantize_mx(
@@ -157,35 +173,39 @@ def tile_modelnew_kernel(tc, x, weight, bn_gamma, bn_beta, bn_mean, bn_var, out_
                 if g == G - 1 and c + 4 < NC:
                     load_w(c + 4)
 
-            def mx(j, h):
-                c, s = divmod(j, 2)
-                cols = slice(P * s, P * (s + 1))
-                a = acc_pool.tile([P, 512], F32, name="acc", tag="acc")
+            def mx(units):
+                accs = [acc_pool.tile([P, 512], F32, name="acc", tag="acc") for u in units]
                 for g in range(G):
-                    nc.tensor.matmul_mx(
-                        out=a[:],
-                        lhsT=wc[c][:, g, cols].bitcast(FP8X4),
-                        lhsT_scale=ws[c][:, g, cols],
-                        rhs=xc[h][:, g, :].bitcast(FP8X4),
-                        rhs_scale=xs[h][:, g, :],
-                        start=(g == 0),
-                        stop=(g == G - 1),
+                    for (j, h), a in zip(units, accs):
+                        c, s = divmod(j, 2)
+                        cols = slice(P * s, P * (s + 1))
+                        nc.tensor.matmul_mx(
+                            out=a[:],
+                            lhsT=wc[c][:, g, cols].bitcast(FP8X4),
+                            lhsT_scale=ws[c][:, g, cols],
+                            rhs=xc[h][:, g, :].bitcast(FP8X4),
+                            rhs_scale=xs[h][:, g, :],
+                            start=(g == 0),
+                            stop=(g == G - 1),
+                        )
+                for (j, h), a in zip(units, accs):
+                    t = g_pool.tile([P, 512], F32, name="gt", tag="gt")
+                    nc.scalar.activation(
+                        out=t[:],
+                        in_=a[:],
+                        func=ACT.Gelu_apprx_tanh,
+                        bias=c_col[:, j : j + 1],
+                        scale=a_col[:, j : j + 1],
                     )
-                t = g_pool.tile([P, 512], F32, name="gt", tag="gt")
-                nc.scalar.activation(
-                    out=t[:],
-                    in_=a[:],
-                    func=ACT.Gelu_apprx_tanh,
-                    bias=c_col[:, j : j + 1],
-                    scale=a_col[:, j : j + 1],
-                )
-                gt[(j, h)] = t
+                    gt[(j, h)] = t
 
             def tr(j, h):
                 c, s = divmod(j, 2)
                 bank = tp_pool.tile([P, 512], F32, name="tp", tag="tp")
                 for q in range(4):
                     nc.tensor.transpose(bank[:, P * q : P * (q + 1)], gt[(j, h)][:, P * q : P * (q + 1)], ident_f[:])
+                k = len(done)
+                done.append((j, h))
                 nc.vector.tensor_scalar(
                     out=out_sb[:, c, 4 * h : 4 * h + 4, P * s : P * (s + 1)],
                     in0=bank[:].rearrange("p (q n) -> p q n", q=4),
@@ -193,9 +213,9 @@ def tile_modelnew_kernel(tc, x, weight, bn_gamma, bn_beta, bn_mean, bn_var, out_
                     scalar2=None,
                     op0=ALU.max,
                     op1=ALU.max,
-                    accum_out=stat[:, 2 * j + h : 2 * j + h + 1],
+                    accum_out=stat[:, k : k + 1],
                 )
-                if s == 1 and h == 1:
+                if len([1 for d in done if d[0] // 2 == c]) == 4:
                     nc.sync.dma_start(out=o0_v[:, :, WC * c : WC * (c + 1)], in_=out_sb[:, c, :, :])
 
             for i in range(4):
@@ -206,63 +226,77 @@ def tile_modelnew_kernel(tc, x, weight, bn_gamma, bn_beta, bn_mean, bn_var, out_
             for c in range(1, 4):
                 load_w(c)
 
+            spin(8)
             prm_ps = tp_pool.tile([P, P], BF16, name="tp", tag="tp")
             nc.tensor.transpose(prm_ps[:], prm[:], ident_b[:])
             nc.vector.tensor_copy(out=prm_t[:], in_=prm_ps[:, 0:64])
             nc.vector.tensor_scalar(out=var_eps[:], in0=prm_t[:, 48:64], scalar1=EPS, scalar2=None, op0=ALU.add)
             nc.gpsimd.tensor_tensor(out=rstd[:], in0=var_eps[:], in1=neg_half[:], op=ALU.pow)
 
-            xt(0)
-            xt(1)
-            xq(0)
-            xt(2)
-            xt(3)
+            xt(0, False)
+            spin(1)
+            xt(1, False)
+            spin(1)
+            for g in range(G):
+                xq(0, g)
+            xt(2, False)
+            spin(1)
+            xt(3, False)
+            spin(8)
             nc.vector.tensor_tensor(out=a_col[:], in0=prm_t[:, 0:16], in1=rstd[:], op=ALU.mult)
-            wcopy(0, 0)
-            wcopy(0, 1)
+            wcopy(0, 0, False)
+            wcopy(0, 1, True)
             nc.vector.tensor_tensor(out=ma_col[:], in0=prm_t[:, 32:48], in1=a_col[:], op=ALU.mult)
-            xq(1)
+            xq(1, 0)
+            xq(1, 1)
             nc.vector.tensor_tensor(out=c_col[:], in0=prm_t[:, 16:32], in1=ma_col[:], op=ALU.subtract)
-            wcopy(0, 2)
+            wcopy(0, 2, False)
             wquant(0, 0)
             wquant(0, 1)
-            wcopy(0, 3)
+            xq(1, 2)
+            xq(1, 3)
+            wcopy(0, 3, True)
             wquant(0, 2)
             wquant(0, 3)
-            mx(0, 0)
-            mx(1, 0)
-            xt(4)
-            xt(5)
+            for i in range(4, NI):
+                xorder(i)
+            mx([(0, 0), (1, 0)])
+            xt(4, True)
+            spin(1)
+            xt(5, True)
+            spin(1)
             wcopy(1, 0, True)
             wcopy(1, 1, True)
-            xq(2)
-            xt(6)
-            xt(7)
+            for g in range(G):
+                xq(2, g)
+            xt(6, True)
+            spin(1)
+            xt(7, True)
+            spin(1)
             wcopy(1, 2, True)
-            xq(3)
+            for g in range(G):
+                xq(3, g)
             wcopy(1, 3, True)
-            wquant(1, 0)
-            wquant(1, 1)
-            wquant(1, 2)
-            wquant(1, 3)
+            for g in range(G):
+                wquant(1, g)
             tr(0, 0)
             tr(1, 0)
-            mx(0, 1)
-            mx(1, 1)
-            wcopy(2, 0)
-            wcopy(2, 1)
+            mx([(0, 1)])
+            mx([(1, 1)])
+            wcopy(2, 0, False)
+            wcopy(2, 1, True)
             for j in range(2, NJ):
-                mx(j, 0)
-                mx(j, 1)
+                mx([(j, 0)])
+                mx([(j, 1)])
                 c = j // 2 + 1
                 if j % 2 == 0:
-                    wcopy(c, 2)
-                    wcopy(c, 3)
+                    wcopy(c, 2, False)
+                    wcopy(c, 3, True)
                     wquant(c, 0)
                     wquant(c, 1)
                 else:
-                    wcopy(c + 1, 0)
-                    wcopy(c + 1, 1)
+                    wcopy(c + 1, 0, False)
+                    wcopy(c + 1, 1, True)
                     wquant(c, 2)
                     wquant(c, 3)
                 if j == 2:

@@ -23,6 +23,8 @@ NI = B // P
 NJ = N // P
 WC = 256
 NC = N // WC
+SW = 512
+NS = N // SW
 
 
 def tile_modelnew_kernel(tc, x, weight, bn_gamma, bn_beta, bn_mean, bn_var, out_0, out_1):
@@ -38,7 +40,7 @@ def tile_modelnew_kernel(tc, x, weight, bn_gamma, bn_beta, bn_mean, bn_var, out_
         tp_pool = ctx.enter_context(tc.psum_pool(name="tpp", bufs=4))
         ctx.enter_context(tc.manual_schedule())
 
-        out_sb = const.tile([P, NC, NI, WC], F32, name="out_sb")
+        out_sb = const.tile([P, NS, NI, SW], F32, name="out_sb")
         stat = const.tile([P, 2 * NJ], F32, name="stat")
         ident_f = const.tile([P, P], F32, name="ident_f")
         ident_b = const.tile([P, P], BF16, name="ident_b")
@@ -56,11 +58,9 @@ def tile_modelnew_kernel(tc, x, weight, bn_gamma, bn_beta, bn_mean, bn_var, out_
         junk = const.tile([P, P], F32, name="junk")
         sfac = const.tile([P, 1], F32, name="sfac")
         rfac = const.tile([P, 1], F32, name="rfac")
-        zero_bf = const.tile([P, 512], BF16, name="zero_bf")
 
         for v, vec in enumerate((bn_gamma, bn_beta, bn_mean, bn_var)):
             nc.sync.dma_start(out=prm[16 * v : 16 * (v + 1), :], in_=vec.rearrange("(j c) -> j c", c=P))
-        nc.vector.memset(zero_bf[:], 0.0)
         nc.vector.memset(warm_in[:], 0.0)
         nc.scalar.activation(out=warm_out[:], in_=warm_in[:], func=ACT.Gelu_apprx_tanh)
         nc.gpsimd.memset(prm[64:128, :], 0.0)
@@ -69,19 +69,17 @@ def tile_modelnew_kernel(tc, x, weight, bn_gamma, bn_beta, bn_mean, bn_var, out_
         nc.gpsimd.memset(neg_half[:], -0.5)
 
         with ExitStack() as ph1:
-            xraw_pool = ph1.enter_context(tc.tile_pool(name="xrawp", bufs=NI))
-            xr_pool = ph1.enter_context(tc.tile_pool(name="xrp", bufs=4))
+            raw_pool = ph1.enter_context(tc.tile_pool(name="rawp", bufs=16))
+            wnarrow_pool = ph1.enter_context(tc.tile_pool(name="wnarrowp", bufs=2 * G))
             xg_pool = ph1.enter_context(tc.tile_pool(name="xgp", bufs=2))
             xc_pool = ph1.enter_context(tc.tile_pool(name="xcp", bufs=1))
-            wraw_pool = ph1.enter_context(tc.tile_pool(name="wrawp", bufs=16))
             wgrp_pool = ph1.enter_context(tc.tile_pool(name="wgrpp", bufs=6))
             wc_pool = ph1.enter_context(tc.tile_pool(name="wcp", bufs=3))
-            g_pool = ph1.enter_context(tc.tile_pool(name="gp", bufs=6))
+            g_pool = ph1.enter_context(tc.tile_pool(name="gp", bufs=8))
 
             xc = [xc_pool.tile([P, G, 512], U32, name="xc%d" % h, align_bytes=64) for h in range(2)]
             xs = [xc_pool.tile([P, G, 512], U8, name="xs%d" % h, align_bytes=64) for h in range(2)]
             xraw = {}
-            xr = {}
             xg = {}
             wraw = {}
             wgrp = {}
@@ -91,30 +89,19 @@ def tile_modelnew_kernel(tc, x, weight, bn_gamma, bn_beta, bn_mean, bn_var, out_
             done = []
 
             def load_x(i):
-                t = xraw_pool.tile([P, K], BF16, name="xraw", tag="xraw")
+                t = raw_pool.tile([P, K], BF16, name="raw", tag="raw")
                 nc.sync.dma_start(out=t[:], in_=x_v[:, i, :])
                 xraw[i] = t
 
-            def load_w(c):
+            def load_w(c, nchunks):
                 for g in range(G):
-                    t = wraw_pool.tile([P, 4, WC], BF16, name="wraw", tag="wraw")
-                    nc.sync.dma_start(out=t[:], in_=w_v[g, :, :, WC * c : WC * (c + 1)])
-                    wraw[(c, g)] = t
-
-            def spin(n):
-                if n == 0:
-                    return
-                t = acc_pool.tile([P, 512], F32, name="acc", tag="acc")
-                for k in range(n):
-                    nc.tensor.matmul(out=t[:], lhsT=zero_bf[:, 0:P], rhs=zero_bf[:], start=True, stop=True)
-
-            def xorder(i):
-                t = xr_pool.tile([P, K // 2], F32, name="xr", tag="xr")
-                nc.vector.tensor_copy(
-                    out=t[:].rearrange("p (g u m) -> p g u m", g=G, u=2),
-                    in_=xraw[i][:].bitcast(F32).rearrange("p (g m u) -> p g u m", g=G, u=2),
-                )
-                xr[i] = t
+                    if nchunks == 1:
+                        t = wnarrow_pool.tile([P, 4, WC], BF16, name="wnarrow", tag="wnarrow")
+                    else:
+                        t = raw_pool.tile([P, 4, 2 * WC], BF16, name="raw", tag="raw")
+                    nc.sync.dma_start(out=t[:], in_=w_v[g, :, :, WC * c : WC * (c + nchunks)])
+                    for k in range(nchunks):
+                        wraw[(c + k, g)] = t[:, :, WC * k : WC * (k + 1)]
 
             def xt(i, both_on_scalar):
                 q, il = divmod(i, 2)
@@ -127,11 +114,9 @@ def tile_modelnew_kernel(tc, x, weight, bn_gamma, bn_beta, bn_mean, bn_var, out_
                         for u in range(2):
                             g = 2 * gp + g2
                             s = 2 * g2 + u
-                            if i in xr:
-                                src_w = xr[i][:, P * (2 * g + u) : P * (2 * g + u + 1)]
-                            else:
-                                src_w = words[:, 256 * g + u : 256 * (g + 1) : 2]
-                            nc.tensor.transpose(bank[:, P * s : P * (s + 1)], src_w, ident_f[:])
+                            nc.tensor.transpose(
+                                bank[:, P * s : P * (s + 1)], words[:, 256 * g + u : 256 * (g + 1) : 2], ident_f[:]
+                            )
                     dst = xg[q][:, 2 * gp : 2 * gp + 2, il, :].bitcast(F32).rearrange("p g (r u) -> p g r u", u=2)
                     src = bank[:].rearrange("p (g u r) -> p g r u", g=2, u=2)
                     if gp == 0 and not both_on_scalar:
@@ -139,20 +124,21 @@ def tile_modelnew_kernel(tc, x, weight, bn_gamma, bn_beta, bn_mean, bn_var, out_
                     else:
                         nc.scalar.copy(out=dst, in_=src)
 
-            def xq(q, g):
+            def xq(q):
                 h, half = divmod(q, 2)
                 cols = slice(256 * half, 256 * (half + 1))
-                nc.vector.quantize_mx(
-                    out=xc[h][:, g, cols].bitcast(FP8X4),
-                    scales=xs[h][:, g, cols],
-                    in_=xg[q][:, g, :, :].rearrange("p l c -> p (l c)"),
-                )
+                for g in range(G):
+                    nc.vector.quantize_mx(
+                        out=xc[h][:, g, cols].bitcast(FP8X4),
+                        scales=xs[h][:, g, cols],
+                        in_=xg[q][:, g, :, :].rearrange("p l c -> p (l c)"),
+                    )
 
             def wcopy(c, g, on_vector):
                 if c >= NC:
                     return
                 t = wgrp_pool.tile([P, WC, 4], BF16, name="wgrp", tag="wgrp", align_bytes=64)
-                src = wraw[(c, g)][:].rearrange("p j n -> p n j")
+                src = wraw[(c, g)].rearrange("p j n -> p n j")
                 if on_vector:
                     nc.vector.tensor_copy(out=t[:], in_=src)
                 else:
@@ -170,44 +156,40 @@ def tile_modelnew_kernel(tc, x, weight, bn_gamma, bn_beta, bn_mean, bn_var, out_
                     scales=ws[c][:, g, :],
                     in_=wgrp[(c, g)][:].rearrange("p n j -> p (n j)"),
                 )
-                if g == G - 1 and c + 4 < NC:
-                    load_w(c + 4)
 
-            def mx(units):
-                accs = [acc_pool.tile([P, 512], F32, name="acc", tag="acc") for u in units]
+            def mx(j, h):
+                c, s = divmod(j, 2)
+                cols = slice(P * s, P * (s + 1))
+                a = acc_pool.tile([P, 512], F32, name="acc", tag="acc")
                 for g in range(G):
-                    for (j, h), a in zip(units, accs):
-                        c, s = divmod(j, 2)
-                        cols = slice(P * s, P * (s + 1))
-                        nc.tensor.matmul_mx(
-                            out=a[:],
-                            lhsT=wc[c][:, g, cols].bitcast(FP8X4),
-                            lhsT_scale=ws[c][:, g, cols],
-                            rhs=xc[h][:, g, :].bitcast(FP8X4),
-                            rhs_scale=xs[h][:, g, :],
-                            start=(g == 0),
-                            stop=(g == G - 1),
-                        )
-                for (j, h), a in zip(units, accs):
-                    t = g_pool.tile([P, 512], F32, name="gt", tag="gt")
-                    nc.scalar.activation(
-                        out=t[:],
-                        in_=a[:],
-                        func=ACT.Gelu_apprx_tanh,
-                        bias=c_col[:, j : j + 1],
-                        scale=a_col[:, j : j + 1],
+                    nc.tensor.matmul_mx(
+                        out=a[:],
+                        lhsT=wc[c][:, g, cols].bitcast(FP8X4),
+                        lhsT_scale=ws[c][:, g, cols],
+                        rhs=xc[h][:, g, :].bitcast(FP8X4),
+                        rhs_scale=xs[h][:, g, :],
+                        start=(g == 0),
+                        stop=(g == G - 1),
                     )
-                    gt[(j, h)] = t
+                t = g_pool.tile([P, 512], F32, name="gt", tag="gt")
+                nc.scalar.activation(
+                    out=t[:],
+                    in_=a[:],
+                    func=ACT.Gelu_apprx_tanh,
+                    bias=c_col[:, j : j + 1],
+                    scale=a_col[:, j : j + 1],
+                )
+                gt[(j, h)] = t
 
             def tr(j, h):
-                c, s = divmod(j, 2)
+                b, s = divmod(j, SW // P)
                 bank = tp_pool.tile([P, 512], F32, name="tp", tag="tp")
                 for q in range(4):
                     nc.tensor.transpose(bank[:, P * q : P * (q + 1)], gt[(j, h)][:, P * q : P * (q + 1)], ident_f[:])
                 k = len(done)
-                done.append((j, h))
+                done.append(b)
                 nc.vector.tensor_scalar(
-                    out=out_sb[:, c, 4 * h : 4 * h + 4, P * s : P * (s + 1)],
+                    out=out_sb[:, b, 4 * h : 4 * h + 4, P * s : P * (s + 1)],
                     in0=bank[:].rearrange("p (q n) -> p q n", q=4),
                     scalar1=0.0,
                     scalar2=None,
@@ -215,18 +197,18 @@ def tile_modelnew_kernel(tc, x, weight, bn_gamma, bn_beta, bn_mean, bn_var, out_
                     op1=ALU.max,
                     accum_out=stat[:, k : k + 1],
                 )
-                if len([1 for d in done if d[0] // 2 == c]) == 4:
-                    nc.sync.dma_start(out=o0_v[:, :, WC * c : WC * (c + 1)], in_=out_sb[:, c, :, :])
+                if len([1 for d in done if d == b]) == 2 * SW // P:
+                    nc.sync.dma_start(out=o0_v[:, :, SW * b : SW * (b + 1)], in_=out_sb[:, b, :, :])
 
             for i in range(4):
                 load_x(i)
-            load_w(0)
+            load_w(0, 1)
             for i in range(4, NI):
                 load_x(i)
-            for c in range(1, 4):
-                load_w(c)
+            load_w(1, 1)
+            load_w(2, 2)
+            load_w(4, 2)
 
-            spin(8)
             prm_ps = tp_pool.tile([P, P], BF16, name="tp", tag="tp")
             nc.tensor.transpose(prm_ps[:], prm[:], ident_b[:])
             nc.vector.tensor_copy(out=prm_t[:], in_=prm_ps[:, 0:64])
@@ -234,79 +216,77 @@ def tile_modelnew_kernel(tc, x, weight, bn_gamma, bn_beta, bn_mean, bn_var, out_
             nc.gpsimd.tensor_tensor(out=rstd[:], in0=var_eps[:], in1=neg_half[:], op=ALU.pow)
 
             xt(0, False)
-            spin(1)
             xt(1, False)
-            spin(1)
-            for g in range(G):
-                xq(0, g)
+            xq(0)
             xt(2, False)
-            spin(1)
             xt(3, False)
-            spin(8)
+            load_w(6, 2)
             nc.vector.tensor_tensor(out=a_col[:], in0=prm_t[:, 0:16], in1=rstd[:], op=ALU.mult)
             wcopy(0, 0, False)
             wcopy(0, 1, True)
             nc.vector.tensor_tensor(out=ma_col[:], in0=prm_t[:, 32:48], in1=a_col[:], op=ALU.mult)
-            xq(1, 0)
-            xq(1, 1)
+            xq(1)
             nc.vector.tensor_tensor(out=c_col[:], in0=prm_t[:, 16:32], in1=ma_col[:], op=ALU.subtract)
             wcopy(0, 2, False)
             wquant(0, 0)
             wquant(0, 1)
-            xq(1, 2)
-            xq(1, 3)
             wcopy(0, 3, True)
             wquant(0, 2)
             wquant(0, 3)
-            for i in range(4, NI):
-                xorder(i)
-            mx([(0, 0), (1, 0)])
+            mx(0, 0)
+            mx(1, 0)
             xt(4, True)
-            spin(1)
             xt(5, True)
-            spin(1)
             wcopy(1, 0, True)
-            wcopy(1, 1, True)
-            for g in range(G):
-                xq(2, g)
+            xq(2)
             xt(6, True)
-            spin(1)
             xt(7, True)
-            spin(1)
-            wcopy(1, 2, True)
-            for g in range(G):
-                xq(3, g)
+            wcopy(1, 1, True)
+            xq(3)
+            wcopy(1, 2, False)
+            wquant(1, 0)
             wcopy(1, 3, True)
-            for g in range(G):
-                wquant(1, g)
+            wquant(1, 1)
+            wquant(1, 2)
+            wquant(1, 3)
             tr(0, 0)
             tr(1, 0)
-            mx([(0, 1)])
-            mx([(1, 1)])
+            mx(0, 1)
             wcopy(2, 0, False)
+            mx(1, 1)
+            wcopy(2, 2, False)
             wcopy(2, 1, True)
-            for j in range(2, NJ):
-                mx([(j, 0)])
-                mx([(j, 1)])
-                c = j // 2 + 1
-                if j % 2 == 0:
-                    wcopy(c, 2, False)
-                    wcopy(c, 3, True)
-                    wquant(c, 0)
-                    wquant(c, 1)
-                else:
-                    wcopy(c + 1, 0, False)
-                    wcopy(c + 1, 1, True)
-                    wquant(c, 2)
-                    wquant(c, 3)
-                if j == 2:
-                    tr(0, 1)
-                    tr(1, 1)
-                else:
-                    tr(j - 1, 0)
-                    tr(j - 1, 1)
-            tr(NJ - 1, 0)
-            tr(NJ - 1, 1)
+            wcopy(2, 3, True)
+            mx(2, 0)
+            wcopy(3, 0, False)
+            mx(2, 1)
+            wcopy(3, 2, False)
+            for g in range(G):
+                wquant(2, g)
+            tr(0, 1)
+            tr(1, 1)
+            wcopy(3, 1, True)
+            wcopy(3, 3, True)
+            for m in range(1, NC - 1):
+                a = 2 * m + 1
+                mx(a, 0)
+                mx(a, 1)
+                wcopy(m + 3, 0, False)
+                mx(a + 1, 0)
+                mx(a + 1, 1)
+                wcopy(m + 3, 2, False)
+                for g in range(G):
+                    wquant(m + 2, g)
+                wcopy(m + 3, 1, True)
+                wcopy(m + 3, 3, True)
+                for j in (a - 1, a):
+                    tr(j, 0)
+                    tr(j, 1)
+            mx(NJ - 1, 0)
+            mx(NJ - 1, 1)
+            for j in (NJ - 2, NJ - 1):
+                tr(j, 0)
+                tr(j, 1)
 
         nc.vector.tensor_reduce(out=pmax[:], in_=stat[:], axis=AX.X, op=ALU.max)
         spread = tp_pool.tile([P, P], F32, name="tp", tag="tp")
@@ -318,70 +298,46 @@ def tile_modelnew_kernel(tc, x, weight, bn_gamma, bn_beta, bn_mean, bn_var, out_
 
         with ExitStack() as ph2:
             sc_pool = ph2.enter_context(tc.tile_pool(name="scp", bufs=3))
-            f8_pool = ph2.enter_context(tc.tile_pool(name="f8p", bufs=NI))
-            f8 = [f8_pool.tile([P, N], FP8, name="f8", tag="f8") for r in range(NI)]
-            work_v = [(r, 0, NC) for r in range(5)] + [(7, 0, 3)]
-            work_s = [(5, 0, NC), (6, 0, NC), (7, 3, NC)]
-            sc_v = {}
-            sc_s = {}
+            f8_pool = ph2.enter_context(tc.tile_pool(name="f8p", bufs=1))
+            work = {True: [(r, 0, NS) for r in range(5)] + [(7, 0, 1)], False: [(5, 0, NS), (6, 0, NS), (7, 1, NS)]}
+            scaled = {}
 
-            def scale_v(k):
-                r, c0, c1 = work_v[k]
-                t = sc_pool.tile([P, (c1 - c0) * WC], F32, name="scv", tag="scv")
-                nc.vector.tensor_scalar(
-                    out=t[:].rearrange("p (c n) -> p c n", n=WC),
-                    in0=out_sb[:, c0:c1, r, :],
-                    scalar1=rfac[:, 0:1],
-                    scalar2=None,
-                    op0=ALU.mult,
-                )
-                sc_v[k] = t
+            def scale(on_vector, k):
+                r, b0, b1 = work[on_vector][k]
+                t = sc_pool.tile([P, (b1 - b0) * SW], F32, name="scv" if on_vector else "scs")
+                dst = t[:].rearrange("p (b n) -> p b n", n=SW)
+                if on_vector:
+                    nc.vector.tensor_scalar(
+                        out=dst, in0=out_sb[:, b0:b1, r, :], scalar1=rfac[:, 0:1], scalar2=None, op0=ALU.mult
+                    )
+                else:
+                    nc.scalar.activation(out=dst, in_=out_sb[:, b0:b1, r, :], func=ACT.Copy, scale=rfac[:, 0:1])
+                scaled[(on_vector, k)] = t
 
-            def scale_s(k):
-                r, c0, c1 = work_s[k]
-                t = sc_pool.tile([P, (c1 - c0) * WC], F32, name="scs", tag="scs")
-                nc.scalar.activation(
-                    out=t[:].rearrange("p (c n) -> p c n", n=WC),
-                    in_=out_sb[:, c0:c1, r, :],
-                    func=ACT.Copy,
-                    scale=rfac[:, 0:1],
-                )
-                sc_s[k] = t
+            def cast(on_vector, k):
+                r, b0, b1 = work[on_vector][k]
+                t = f8_pool.tile([P, (b1 - b0) * SW], FP8, name="f8_%d_%d" % (r, b0))
+                if on_vector:
+                    nc.vector.tensor_copy(out=t[:], in_=scaled[(on_vector, k)][:], saturate=False)
+                else:
+                    nc.scalar.copy(out=t[:], in_=scaled[(on_vector, k)][:], saturate=False)
+                nc.sync.dma_start(out=o1_v[:, N * r + SW * b0 : N * r + SW * b1], in_=t[:].bitcast(U8))
 
-            def cast_v(k):
-                r, c0, c1 = work_v[k]
-                nc.vector.tensor_copy(out=f8[r][:, WC * c0 : WC * c1], in_=sc_v[k][:], saturate=False)
-
-            def cast_s(k):
-                r, c0, c1 = work_s[k]
-                nc.scalar.copy(out=f8[r][:, WC * c0 : WC * c1], in_=sc_s[k][:], saturate=False)
-
-            def store1(r):
-                nc.sync.dma_start(out=o1_v[:, N * r : N * (r + 1)], in_=f8[r][:].bitcast(U8))
-
-            scale_v(0)
-            scale_s(0)
-            scale_v(1)
-            cast_v(0)
-            store1(0)
-            scale_s(1)
-            scale_v(2)
-            cast_v(1)
-            store1(1)
-            cast_s(0)
-            store1(5)
-            scale_v(3)
-            cast_v(2)
-            store1(2)
-            scale_s(2)
-            scale_v(4)
-            cast_v(3)
-            store1(3)
-            cast_s(1)
-            store1(6)
-            scale_v(5)
-            cast_v(4)
-            store1(4)
-            cast_s(2)
-            cast_v(5)
-            store1(7)
+            scale(True, 0)
+            scale(False, 0)
+            scale(True, 1)
+            cast(True, 0)
+            scale(False, 1)
+            scale(True, 2)
+            cast(True, 1)
+            cast(False, 0)
+            scale(True, 3)
+            cast(True, 2)
+            scale(False, 2)
+            scale(True, 4)
+            cast(True, 3)
+            cast(False, 1)
+            scale(True, 5)
+            cast(True, 4)
+            cast(True, 5)
+            cast(False, 2)

@@ -200,6 +200,22 @@ def tile_modelnew_kernel(tc, x, weight, bn_gamma, bn_beta, bn_mean, bn_var, out_
                 if len([1 for d in done if d == b]) == 2 * SW // P:
                     nc.sync.dma_start(out=o0_v[:, :, SW * b : SW * (b + 1)], in_=out_sb[:, b, :, :])
 
+
+            def gmax(j, h):
+                nc.vector.tensor_reduce(out=stat[:, len(done) + 2 * (j - NJ + 2) + h : len(done) + 2 * (j - NJ + 2) + h + 1], in_=gt[(j, h)][:], axis=AX.X, op=ALU.max)
+
+            def tr_late(j, h, on_vector):
+                b, s = divmod(j, SW // P)
+                bank = tp_pool.tile([P, 512], F32, name="tp", tag="tp")
+                for q in range(4):
+                    nc.tensor.transpose(bank[:, P * q : P * (q + 1)], gt[(j, h)][:, P * q : P * (q + 1)], ident_f[:])
+                dst = out_sb[:, b, 4 * h : 4 * h + 4, P * s : P * (s + 1)]
+                src = bank[:].rearrange("p (q n) -> p q n", q=4)
+                if on_vector:
+                    nc.vector.tensor_scalar(out=dst, in0=src, scalar1=0.0, scalar2=None, op0=ALU.max)
+                else:
+                    nc.scalar.activation(out=dst, in_=src, func=ACT.Relu)
+
             for i in range(4):
                 load_x(i)
             load_w(0, 1)
@@ -282,13 +298,19 @@ def tile_modelnew_kernel(tc, x, weight, bn_gamma, bn_beta, bn_mean, bn_var, out_
                 for j in (a - 1, a):
                     tr(j, 0)
                     tr(j, 1)
+            gmax(NJ - 2, 0)
+            gmax(NJ - 2, 1)
             mx(NJ - 1, 0)
+            gmax(NJ - 1, 0)
             mx(NJ - 1, 1)
-            for j in (NJ - 2, NJ - 1):
-                tr(j, 0)
-                tr(j, 1)
+            gmax(NJ - 1, 1)
+            nc.vector.tensor_reduce(out=pmax[:], in_=stat[:], axis=AX.X, op=ALU.max)
+            tr_late(NJ - 2, 0, False)
+            tr_late(NJ - 2, 1, False)
+            tr_late(NJ - 1, 0, False)
+            tr_late(NJ - 1, 1, True)
+            nc.sync.dma_start(out=o0_v[:, :, SW * (NS - 1) : N], in_=out_sb[:, NS - 1, :, :])
 
-        nc.vector.tensor_reduce(out=pmax[:], in_=stat[:], axis=AX.X, op=ALU.max)
         spread = tp_pool.tile([P, P], F32, name="tp", tag="tp")
         nc.tensor.transpose(spread[:], pmax[:, 0:1].to_broadcast([P, P]), ident_f[:])
         nc.vector.tensor_scalar(

from contextlib import ExitStack

import concourse.masks as masks
import concourse.mybir as mybir

B, K, N = 1024, 2048, 2048
EPS = 1e-5
FLOPS = 2 * B * K * N

F32 = mybir.dt.float32
BF16 = mybir.dt.bfloat16
U32 = mybir.dt.uint32
U8 = mybir.dt.uint8
FP8X4 = mybir.dt.float8_e4m3fn_x4
FP8 = mybir.dt.float8_e4m3fn
ALU = mybir.AluOpType
ACT = mybir.ActivationFunctionType
AX = mybir.AxisListType

P = 128
G = K // 512
NI = B // P
NJ = N // P
WC = 256
NC = N // WC
SW = 512
NS = N // SW


def tile_modelnew_kernel(tc, x, weight, bn_gamma, bn_beta, bn_mean, bn_var, out_0, out_1):
    nc = tc.nc
    x_v = x.rearrange("(p i) k -> p i k", i=NI)
    w_v = weight.rearrange("(g p j) n -> g p j n", g=G, j=4)
    o0_v = out_0.rearrange("(p i) n -> p i n", i=NI)
    o1_v = out_1.rearrange("(p i) n -> p (i n)", i=NI)

    with ExitStack() as ctx:
        const = ctx.enter_context(tc.tile_pool(name="const", bufs=1))
        acc_pool = ctx.enter_context(tc.psum_pool(name="accp", bufs=4))
        tp_pool = ctx.enter_context(tc.psum_pool(name="tpp", bufs=4))
        ctx.enter_context(tc.manual_schedule())

        out_sb = const.tile([P, NS, NI, SW], F32, name="out_sb")
        stat = const.tile([P, 2 * NJ], F32, name="stat")
        ident_f = const.tile([P, P], F32, name="ident_f")
        ident_b = const.tile([P, P], BF16, name="ident_b")
        prm = const.tile([P, P], BF16, name="prm")
        prm_t = const.tile([P, 64], F32, name="prm_t")
        neg_half = const.tile([P, NJ], F32, name="neg_half")
        var_eps = const.tile([P, NJ], F32, name="var_eps")
        rstd = const.tile([P, NJ], F32, name="rstd")
        a_col = const.tile([P, NJ], F32, name="a_col")
        ma_col = const.tile([P, NJ], F32, name="ma_col")
        c_col = const.tile([P, NJ], F32, name="c_col")
        warm_in = const.tile([P, 1], F32, name="warm_in")
        warm_out = const.tile([P, 1], F32, name="warm_out")
        pmax = const.tile([P, 1], F32, name="pmax")
        junk = const.tile([P, P], F32, name="junk")
        sfac = const.tile([P, 1], F32, name="sfac")
        rfac = const.tile([P, 1], F32, name="rfac")

        for v, vec in enumerate((bn_gamma, bn_beta, bn_mean, bn_var)):
            nc.sync.dma_start(out=prm[16 * v : 16 * (v + 1), :], in_=vec.rearrange("(j c) -> j c", c=P))
        nc.vector.memset(warm_in[:], 0.0)
        nc.scalar.activation(out=warm_out[:], in_=warm_in[:], func=ACT.Gelu_apprx_tanh)
        nc.gpsimd.memset(prm[64:128, :], 0.0)
        masks.make_identity(nc, ident_b[:])
        masks.make_identity(nc, ident_f[:])
        nc.gpsimd.memset(neg_half[:], -0.5)

        with ExitStack() as ph1:
            raw_pool = ph1.enter_context(tc.tile_pool(name="rawp", bufs=16))
            wnarrow_pool = ph1.enter_context(tc.tile_pool(name="wnarrowp", bufs=2 * G))
            xg_pool = ph1.enter_context(tc.tile_pool(name="xgp", bufs=2))
            xc_pool = ph1.enter_context(tc.tile_pool(name="xcp", bufs=1))
            wgrp_pool = ph1.enter_context(tc.tile_pool(name="wgrpp", bufs=6))
            wc_pool = ph1.enter_context(tc.tile_pool(name="wcp", bufs=3))
            g_pool = ph1.enter_context(tc.tile_pool(name="gp", bufs=8))

            xc = [xc_pool.tile([P, G, 512], U32, name="xc%d" % h, align_bytes=64) for h in range(2)]
            xs = [xc_pool.tile([P, G, 512], U8, name="xs%d" % h, align_bytes=64) for h in range(2)]
            xraw = {}
            xg = {}
            wraw = {}
            wgrp = {}
            wc = {}
            ws = {}
            gt = {}
            done = []

            def load_x(i):
                t = raw_pool.tile([P, K], BF16, name="raw", tag="raw")
                nc.sync.dma_start(out=t[:], in_=x_v[:, i, :])
                xraw[i] = t

            def load_w(c, nchunks):
                for g in range(G):
                    if nchunks == 1:
                        t = wnarrow_pool.tile([P, 4, WC], BF16, name="wnarrow", tag="wnarrow")
                    else:
                        t = raw_pool.tile([P, 4, 2 * WC], BF16, name="raw", tag="raw")
                    nc.sync.dma_start(out=t[:], in_=w_v[g, :, :, WC * c : WC * (c + nchunks)])
                    for k in range(nchunks):
                        wraw[(c + k, g)] = t[:, :, WC * k : WC * (k + 1)]

            def xt(i, both_on_scalar):
                q, il = divmod(i, 2)
                if il == 0:
                    xg[q] = xg_pool.tile([P, G, 2, 512], BF16, name="xg", tag="xg", align_bytes=64)
                words = xraw[i][:].bitcast(F32)
                for gp in range(2):
                    bank = tp_pool.tile([P, 512], F32, name="tp", tag="tp")
                    for g2 in range(2):
                        for u in range(2):
                            g = 2 * gp + g2
                            s = 2 * g2 + u
                            nc.tensor.transpose(
                                bank[:, P * s : P * (s + 1)], words[:, 256 * g + u : 256 * (g + 1) : 2], ident_f[:]
                            )
                    dst = xg[q][:, 2 * gp : 2 * gp + 2, il, :].bitcast(F32).rearrange("p g (r u) -> p g r u", u=2)
                    src = bank[:].rearrange("p (g u r) -> p g r u", g=2, u=2)
                    if gp == 0 and not both_on_scalar:
                        nc.vector.tensor_copy(out=dst, in_=src)
                    else:
                        nc.scalar.copy(out=dst, in_=src)

            def xq(q):
                h, half = divmod(q, 2)
                cols = slice(256 * half, 256 * (half + 1))
                for g in range(G):
                    nc.vector.quantize_mx(
                        out=xc[h][:, g, cols].bitcast(FP8X4),
                        scales=xs[h][:, g, cols],
                        in_=xg[q][:, g, :, :].rearrange("p l c -> p (l c)"),
                    )

            def wcopy(c, g, on_vector):
                if c >= NC:
                    return
                t = wgrp_pool.tile([P, WC, 4], BF16, name="wgrp", tag="wgrp", align_bytes=64)
                src = wraw[(c, g)].rearrange("p j n -> p n j")
                if on_vector:
                    nc.vector.tensor_copy(out=t[:], in_=src)
                else:
                    nc.scalar.copy(out=t[:], in_=src)
                wgrp[(c, g)] = t

            def wquant(c, g):
                if c >= NC:
                    return
                if c not in wc:
                    wc[c] = wc_pool.tile([P, G, WC], U32, name="wc", tag="wc", align_bytes=64)
                    ws[c] = wc_pool.tile([P, G, WC], U8, name="ws", tag="ws", align_bytes=64)
                nc.vector.quantize_mx(
                    out=wc[c][:, g, :].bitcast(FP8X4),
                    scales=ws[c][:, g, :],
                    in_=wgrp[(c, g)][:].rearrange("p n j -> p (n j)"),
                )

            def mx(j, h):
                c, s = divmod(j, 2)
                cols = slice(P * s, P * (s + 1))
                a = acc_pool.tile([P, 512], F32, name="acc", tag="acc")
                for g in range(G):
                    nc.tensor.matmul_mx(
                        out=a[:],
                        lhsT=wc[c][:, g, cols].bitcast(FP8X4),
                        lhsT_scale=ws[c][:, g, cols],
                        rhs=xc[h][:, g, :].bitcast(FP8X4),
                        rhs_scale=xs[h][:, g, :],
                        start=(g == 0),
                        stop=(g == G - 1),
                    )
                t = g_pool.tile([P, 512], F32, name="gt", tag="gt")
                nc.scalar.activation(
                    out=t[:],
                    in_=a[:],
                    func=ACT.Gelu_apprx_tanh,
                    bias=c_col[:, j : j + 1],
                    scale=a_col[:, j : j + 1],
                )
                gt[(j, h)] = t

            def tr(j, h):
                b, s = divmod(j, SW // P)
                bank = tp_pool.tile([P, 512], F32, name="tp", tag="tp")
                for q in range(4):
                    nc.tensor.transpose(bank[:, P * q : P * (q + 1)], gt[(j, h)][:, P * q : P * (q + 1)], ident_f[:])
                k = len(done)
                done.append(b)
                nc.vector.tensor_scalar(
                    out=out_sb[:, b, 4 * h : 4 * h + 4, P * s : P * (s + 1)],
                    in0=bank[:].rearrange("p (q n) -> p q n", q=4),
                    scalar1=0.0,
                    scalar2=None,
                    op0=ALU.max,
                    op1=ALU.max,
                    accum_out=stat[:, k : k + 1],
                )
                if len([1 for d in done if d == b]) == 2 * SW // P:
                    nc.sync.dma_start(out=o0_v[:, :, SW * b : SW * (b + 1)], in_=out_sb[:, b, :, :])


            def gmax(j, h):
                nc.vector.tensor_reduce(out=stat[:, len(done) + 2 * (j - NJ + 2) + h : len(done) + 2 * (j - NJ + 2) + h + 1], in_=gt[(j, h)][:], axis=AX.X, op=ALU.max)

            def tr_late(j, h, on_vector):
                b, s = divmod(j, SW // P)
                bank = tp_pool.tile([P, 512], F32, name="tp", tag="tp")
                for q in range(4):
                    nc.tensor.transpose(bank[:, P * q : P * (q + 1)], gt[(j, h)][:, P * q : P * (q + 1)], ident_f[:])
                dst = out_sb[:, b, 4 * h : 4 * h + 4, P * s : P * (s + 1)]
                src = bank[:].rearrange("p (q n) -> p q n", q=4)
                if on_vector:
                    nc.vector.tensor_scalar(out=dst, in0=src, scalar1=0.0, scalar2=None, op0=ALU.max)
                else:
                    nc.scalar.activation(out=dst, in_=src, func=ACT.Relu)

            for i in range(4):
                load_x(i)
            load_w(0, 1)
            for i in range(4, NI):
                load_x(i)
            load_w(1, 1)
            load_w(2, 2)
            load_w(4, 2)

            prm_ps = tp_pool.tile([P, P], BF16, name="tp", tag="tp")
            nc.tensor.transpose(prm_ps[:], prm[:], ident_b[:])
            nc.vector.tensor_copy(out=prm_t[:], in_=prm_ps[:, 0:64])
            nc.vector.tensor_scalar(out=var_eps[:], in0=prm_t[:, 48:64], scalar1=EPS, scalar2=None, op0=ALU.add)
            nc.gpsimd.tensor_tensor(out=rstd[:], in0=var_eps[:], in1=neg_half[:], op=ALU.pow)

            xt(0, False)
            xt(1, False)
            xq(0)
            xt(2, False)
            xt(3, False)
            load_w(6, 2)
            nc.vector.tensor_tensor(out=a_col[:], in0=prm_t[:, 0:16], in1=rstd[:], op=ALU.mult)
            wcopy(0, 0, False)
            wcopy(0, 1, True)
            nc.vector.tensor_tensor(out=ma_col[:], in0=prm_t[:, 32:48], in1=a_col[:], op=ALU.mult)
            xq(1)
            nc.vector.tensor_tensor(out=c_col[:], in0=prm_t[:, 16:32], in1=ma_col[:], op=ALU.subtract)
            wcopy(0, 2, False)
            wquant(0, 0)
            wquant(0, 1)
            wcopy(0, 3, True)
            wquant(0, 2)
            wquant(0, 3)
            mx(0, 0)
            mx(1, 0)
            xt(4, True)
            xt(5, True)
            wcopy(1, 0, True)
            xq(2)
            xt(6, True)
            xt(7, True)
            wcopy(1, 1, True)
            xq(3)
            wcopy(1, 2, False)
            wquant(1, 0)
            wcopy(1, 3, True)
            wquant(1, 1)
            wquant(1, 2)
            wquant(1, 3)
            tr(0, 0)
            tr(1, 0)
            mx(0, 1)
            wcopy(2, 0, False)
            mx(1, 1)
            wcopy(2, 2, False)
            wcopy(2, 1, True)
            wcopy(2, 3, True)
            mx(2, 0)
            wcopy(3, 0, False)
            mx(2, 1)
            wcopy(3, 2, False)
            for g in range(G):
                wquant(2, g)
            tr(0, 1)
            tr(1, 1)
            wcopy(3, 1, True)
            wcopy(3, 3, True)
            for m in range(1, NC - 1):
                a = 2 * m + 1
                mx(a, 0)
                mx(a, 1)
                wcopy(m + 3, 0, False)
                mx(a + 1, 0)
                mx(a + 1, 1)
                wcopy(m + 3, 2, False)
                for g in range(G):
                    wquant(m + 2, g)
                wcopy(m + 3, 1, True)
                wcopy(m + 3, 3, True)
                for j in (a - 1, a):
                    tr(j, 0)
                    tr(j, 1)
            gmax(NJ - 2, 0)
            gmax(NJ - 2, 1)
            mx(NJ - 1, 0)
            gmax(NJ - 1, 0)
            mx(NJ - 1, 1)
            gmax(NJ - 1, 1)
            nc.vector.tensor_reduce(out=pmax[:], in_=stat[:], axis=AX.X, op=ALU.max)
            tr_late(NJ - 2, 0, False)
            tr_late(NJ - 2, 1, False)
            tr_late(NJ - 1, 0, False)
            tr_late(NJ - 1, 1, True)
            nc.sync.dma_start(out=o0_v[:, :, SW * (NS - 1) : N], in_=out_sb[:, NS - 1, :, :])

        spread = tp_pool.tile([P, P], F32, name="tp", tag="tp")
        nc.tensor.transpose(spread[:], pmax[:, 0:1].to_broadcast([P, P]), ident_f[:])
        nc.vector.tensor_scalar(
            out=junk[:], in0=spread[:], scalar1=1.0 / 448.0, scalar2=None, op0=ALU.mult, op1=ALU.max, accum_out=sfac[:]
        )
        nc.vector.reciprocal(out=rfac[:], in_=sfac[:])

        with ExitStack() as ph2:
            sc_pool = ph2.enter_context(tc.tile_pool(name="scp", bufs=3))
            f8_pool = ph2.enter_context(tc.tile_pool(name="f8p", bufs=1))
            work = {True: [(r, 0, NS) for r in range(5)] + [(7, 0, 1)], False: [(5, 0, NS), (6, 0, NS), (7, 1, NS)]}
            scaled = {}

            def scale(on_vector, k):
                r, b0, b1 = work[on_vector][k]
                t = sc_pool.tile([P, (b1 - b0) * SW], F32, name="scv" if on_vector else "scs")
                dst = t[:].rearrange("p (b n) -> p b n", n=SW)
                if on_vector:
                    nc.vector.tensor_scalar(
                        out=dst, in0=out_sb[:, b0:b1, r, :], scalar1=rfac[:, 0:1], scalar2=None, op0=ALU.mult
                    )
                else:
                    nc.scalar.activation(out=dst, in_=out_sb[:, b0:b1, r, :], func=ACT.Copy, scale=rfac[:, 0:1])
                scaled[(on_vector, k)] = t

            def cast(on_vector, k):
                r, b0, b1 = work[on_vector][k]
                t = f8_pool.tile([P, (b1 - b0) * SW], FP8, name="f8_%d_%d" % (r, b0))
                if on_vector:
                    nc.vector.tensor_copy(out=t[:], in_=scaled[(on_vector, k)][:], saturate=False)
                else:
                    nc.scalar.copy(out=t[:], in_=scaled[(on_vector, k)][:], saturate=False)
                nc.sync.dma_start(out=o1_v[:, N * r + SW * b0 : N * r + SW * b1], in_=t[:].bitcast(U8))

            scale(True, 0)
            scale(False, 0)
            scale(True, 1)
            cast(True, 0)
            scale(False, 1)
            scale(True, 2)
            cast(True, 1)
            cast(False, 0)
            scale(True, 3)
            cast(True, 2)
            scale(False, 2)
            scale(True, 4)
            cast(True, 3)
            cast(False, 1)
            scale(True, 5)
            cast(True, 4)
            cast(True, 5)
            cast(False, 2)
